import numpy as np
import ml_dtypes

BF16 = ml_dtypes.bfloat16


def bf(x):
    return np.asarray(x, np.float32).astype(BF16)


def f32(x):
    return np.asarray(x, np.float32)


def f64(x):
    return np.asarray(x).astype(np.float64)


def striped(idx):
    return np.tile(idx.reshape(-1, 16).T, (8, 1))


E, NF, H, C, S, N = 128, 128, 256, 768, 512, 256
CLIP, WMAX, WMIN, PEAK = 3.0, 0.5, 1e-4, 4.0


def sigmoid(v):
    return 1.0 / (1.0 + np.exp(-v))


def setup_inputs():
    z = PEAK * np.random.standard_normal((NF, N))
    r = np.exp(z - z.max(axis=0, keepdims=True))
    r = r / r.sum(axis=0, keepdims=True)
    wgt = (1.0 - NF * WMIN) * r + WMIN
    return {"emb": f32(2.0 * np.random.standard_normal((E, S))), "w_emb": bf(0.6 * np.random.standard_normal((E, C)) / np.sqrt(E)), "sf": f32(2.0 * np.random.standard_normal((NF, N))), "wgt": f32(wgt), "w_feat": bf(np.random.standard_normal((NF, C))), "b": f32(0.3 * np.random.standard_normal((C, 1))), "offs": striped(np.random.permutation(np.tile(np.arange(S), 2))[:N])}


def reference(emb, w_emb, sf, wgt, w_feat, b, offs):
    idx = offs[:16].T.reshape(-1)
    proj = f64(w_emb).T @ np.clip(f64(emb), -CLIP, CLIP)
    wf = np.clip(f64(sf), -CLIP, CLIP) * np.minimum(f64(wgt), WMAX)
    q = f64(w_feat).T @ wf + f64(b)
    a = proj[:, idx] + q
    a_in, a_cand, a_out = np.split(a, C // H, axis=0)
    return sigmoid(a_out) * np.tanh(sigmoid(a_in) * np.tanh(a_cand))

@@ -1,0 +1,93 @@
+import concourse.mybir as mybir
+from concourse.masks import make_identity
+
+F32 = mybir.dt.float32
+BF16 = mybir.dt.bfloat16
+U16 = mybir.dt.uint16
+ALU = mybir.AluOpType
+ACT = mybir.ActivationFunctionType
+
+P = 128
+HIDDEN = 256
+GATES = 3
+BASINS = 512
+SAMPLES = 256
+HALVES = HIDDEN // P
+BLOCKS = GATES * HALVES
+CLIP = 3.0
+WEIGHT_CAP = 0.5
+
+FLOPS = 2 * P * GATES * HIDDEN * (BASINS + SAMPLES)
+
+
+def tile_sca2lstm_kernel(tc, emb, w_emb, sf, wgt, w_feat, b, offs, out):
+    nc = tc.nc
+    with (
+        tc.tile_pool(name="held", bufs=1) as held,
+        tc.tile_pool(name="work", bufs=2) as work,
+        tc.psum_pool(name="proj_banks", bufs=4) as proj_banks,
+        tc.psum_pool(name="q_banks", bufs=3) as q_banks,
+        tc.psum_pool(name="bias_bank", bufs=1) as bias_bank,
+    ):
+        emb_f32 = held.tile([P, BASINS], F32, name="emb_f32")
+        nc.sync.dma_start(emb_f32[:], emb)
+        w_emb_sb = held.tile([P, BLOCKS * P], BF16, name="w_emb_sb")
+        nc.scalar.dma_start(w_emb_sb[:], w_emb)
+        sf_f32 = held.tile([P, SAMPLES], F32, name="sf_f32")
+        nc.sync.dma_start(sf_f32[:], sf)
+        wgt_f32 = held.tile([P, SAMPLES], F32, name="wgt_f32")
+        nc.scalar.dma_start(wgt_f32[:], wgt)
+        w_feat_sb = held.tile([P, BLOCKS * P], BF16, name="w_feat_sb")
+        nc.scalar.dma_start(w_feat_sb[:], w_feat)
+        b_rows = held.tile([BLOCKS, P], F32, name="b_rows")
+        nc.sync.dma_start(b_rows[:], b.rearrange("(k p) o -> k (p o)", p=P))
+        offsets = held.tile([P, SAMPLES // 16], U16, name="offsets")
+        nc.sync.dma_start(offsets[:], offs)
+
+        scratch_in = held.tile([P, 1], F32, name="scratch_in")
+        scratch_out = held.tile([P, 1], F32, name="scratch_out")
+        nc.vector.memset(scratch_in[:], 0.0)
+        nc.scalar.activation(scratch_out[:], scratch_in[:], ACT.Sigmoid)
+
+        emb_bf = held.tile([P, BASINS], BF16, name="emb_bf")
+        nc.vector.tensor_scalar(emb_bf[:], emb_f32[:], -CLIP, CLIP, ALU.max, ALU.min)
+        sf_clipped = held.tile([P, SAMPLES], F32, name="sf_clipped")
+        nc.gpsimd.tensor_scalar(sf_clipped[:], sf_f32[:], -CLIP, CLIP, ALU.max, ALU.min)
+        wf_bf = held.tile([P, SAMPLES], BF16, name="wf_bf")
+        nc.vector.scalar_tensor_tensor(
+            wf_bf[:], wgt_f32[:], WEIGHT_CAP, sf_clipped[:], ALU.min, ALU.mult
+        )
+
+        identity = held.tile([BLOCKS, BLOCKS], F32, name="identity")
+        make_identity(nc, identity[:])
+        bias_ps = bias_bank.tile([P, BLOCKS], F32, name="bias_ps")
+        nc.tensor.matmul(bias_ps[:], b_rows[:], identity[:], start=True, stop=True)
+        bias = held.tile([P, BLOCKS], F32, name="bias")
+        nc.vector.tensor_copy(bias[:], bias_ps[:])
+
+        functions = (ACT.Sigmoid, ACT.Tanh, ACT.Sigmoid)
+        for half in range(HALVES):
+            gate = []
+            for g in range(GATES):
+                block = g * HALVES + half
+                rows = slice(block * P, (block + 1) * P)
+                proj_ps = proj_banks.tile([P, BASINS], F32, name="proj_ps")
+                nc.tensor.matmul(proj_ps[:], w_emb_sb[:, rows], emb_bf[:], start=True, stop=True)
+                proj = held.tile([P, BASINS], F32, name=f"proj{block}")
+                nc.scalar.copy(proj[:], proj_ps[:])
+                q_ps = q_banks.tile([P, SAMPLES], F32, name="q_ps")
+                nc.tensor.matmul(q_ps[:], w_feat_sb[:, rows], wf_bf[:], start=True, stop=True)
+                q = work.tile([P, SAMPLES], F32, name=f"q{g}")
+                nc.vector.tensor_scalar_add(q[:], q_ps[:], bias[:, block : block + 1])
+                a = work.tile([P, SAMPLES], F32, name=f"a{g}")
+                nc.vector.tensor_tensor(a[:], proj[:].indirect(offsets[:]), q[:], ALU.add)
+                acted = work.tile([P, SAMPLES], F32, name=f"gate{g}")
+                nc.scalar.activation(acted[:], a[:], functions[g])
+                gate.append(acted)
+            cell = work.tile([P, SAMPLES], F32, name="cell")
+            nc.gpsimd.tensor_tensor(cell[:], gate[0][:], gate[1][:], ALU.mult)
+            cell_tanh = work.tile([P, SAMPLES], F32, name="cell_tanh")
+            nc.scalar.activation(cell_tanh[:], cell[:], ACT.Tanh)
+            hidden = work.tile([P, SAMPLES], F32, name="hidden")
+            nc.vector.tensor_tensor(hidden[:], gate[2][:], cell_tanh[:], ALU.mult)
+            nc.sync.dma_start(out[half * P : (half + 1) * P, :], hidden[:])

@@ -10,10 +10,13 @@ ACT = mybir.ActivationFunctionType
 P = 128
 HIDDEN = 256
 GATES = 3
+INPUT, CANDIDATE, OUTPUT = 0, 1, 2
 BASINS = 512
 SAMPLES = 256
 HALVES = HIDDEN // P
 BLOCKS = GATES * HALVES
+PSUM_BANKS = 8
+WARM_MATMULS = 6
 CLIP = 3.0
 WEIGHT_CAP = 0.5
 
@@ -24,35 +27,37 @@ def tile_sca2lstm_kernel(tc, emb, w_emb, sf, wgt, w_feat, b, offs, out):
     nc = tc.nc
     with (
         tc.tile_pool(name="held", bufs=1) as held,
-        tc.tile_pool(name="work", bufs=2) as work,
-        tc.psum_pool(name="proj_banks", bufs=4) as proj_banks,
-        tc.psum_pool(name="q_banks", bufs=3) as q_banks,
-        tc.psum_pool(name="bias_bank", bufs=1) as bias_bank,
+        tc.psum_pool(name="banks", bufs=PSUM_BANKS) as banks,
     ):
         emb_f32 = held.tile([P, BASINS], F32, name="emb_f32")
         nc.sync.dma_start(emb_f32[:], emb)
-        w_emb_sb = held.tile([P, BLOCKS * P], BF16, name="w_emb_sb")
-        nc.scalar.dma_start(w_emb_sb[:], w_emb)
         sf_f32 = held.tile([P, SAMPLES], F32, name="sf_f32")
-        nc.sync.dma_start(sf_f32[:], sf)
+        nc.scalar.dma_start(sf_f32[:], sf)
+        b_rows = held.tile([BLOCKS, P], F32, name="b_rows")
+        nc.gpsimd.dma_start(b_rows[:], b.rearrange("(k p) o -> k (p o)", p=P))
+        w_emb_sb = held.tile([P, BLOCKS * P], BF16, name="w_emb_sb")
+        nc.sync.dma_start(w_emb_sb[:], w_emb)
         wgt_f32 = held.tile([P, SAMPLES], F32, name="wgt_f32")
         nc.scalar.dma_start(wgt_f32[:], wgt)
-        w_feat_sb = held.tile([P, BLOCKS * P], BF16, name="w_feat_sb")
-        nc.scalar.dma_start(w_feat_sb[:], w_feat)
-        b_rows = held.tile([BLOCKS, P], F32, name="b_rows")
-        nc.sync.dma_start(b_rows[:], b.rearrange("(k p) o -> k (p o)", p=P))
         offsets = held.tile([P, SAMPLES // 16], U16, name="offsets")
         nc.sync.dma_start(offsets[:], offs)
+        w_feat_sb = held.tile([P, BLOCKS * P], BF16, name="w_feat_sb")
+        nc.scalar.dma_start(w_feat_sb[:], w_feat)
 
         scratch_in = held.tile([P, 1], F32, name="scratch_in")
         scratch_out = held.tile([P, 1], F32, name="scratch_out")
         nc.vector.memset(scratch_in[:], 0.0)
         nc.scalar.activation(scratch_out[:], scratch_in[:], ACT.Sigmoid)
+        zeros = held.tile([P, BASINS], BF16, name="zeros")
+        nc.vector.memset(zeros[:], 0.0)
+        unread_ps = banks.tile([P, BASINS], F32, name="unread_ps", tag="bank")
+        for repeat in range(WARM_MATMULS):
+            nc.tensor.matmul(unread_ps[:], zeros[:, 0:P], zeros[:], start=True, stop=True)
 
+        sf_clipped = held.tile([P, SAMPLES], F32, name="sf_clipped")
+        nc.vector.tensor_scalar(sf_clipped[:], sf_f32[:], -CLIP, CLIP, ALU.max, ALU.min)
         emb_bf = held.tile([P, BASINS], BF16, name="emb_bf")
         nc.vector.tensor_scalar(emb_bf[:], emb_f32[:], -CLIP, CLIP, ALU.max, ALU.min)
-        sf_clipped = held.tile([P, SAMPLES], F32, name="sf_clipped")
-        nc.gpsimd.tensor_scalar(sf_clipped[:], sf_f32[:], -CLIP, CLIP, ALU.max, ALU.min)
         wf_bf = held.tile([P, SAMPLES], BF16, name="wf_bf")
         nc.vector.scalar_tensor_tensor(
             wf_bf[:], wgt_f32[:], WEIGHT_CAP, sf_clipped[:], ALU.min, ALU.mult
@@ -60,34 +65,54 @@ def tile_sca2lstm_kernel(tc, emb, w_emb, sf, wgt, w_feat, b, offs, out):
 
         identity = held.tile([BLOCKS, BLOCKS], F32, name="identity")
         make_identity(nc, identity[:])
-        bias_ps = bias_bank.tile([P, BLOCKS], F32, name="bias_ps")
+        bias_ps = banks.tile([P, BLOCKS], F32, name="bias_ps", tag="bank")
         nc.tensor.matmul(bias_ps[:], b_rows[:], identity[:], start=True, stop=True)
         bias = held.tile([P, BLOCKS], F32, name="bias")
         nc.vector.tensor_copy(bias[:], bias_ps[:])
 
-        functions = (ACT.Sigmoid, ACT.Tanh, ACT.Sigmoid)
-        for half in range(HALVES):
-            gate = []
-            for g in range(GATES):
+        order = [(g, half) for half in range(HALVES) for g in (INPUT, CANDIDATE)]
+        order += [(OUTPUT, half) for half in range(HALVES)]
+        functions = {INPUT: ACT.Sigmoid, CANDIDATE: ACT.Tanh, OUTPUT: ACT.Sigmoid}
+        proj, q, a, gate, cell_tanh = {}, {}, {}, {}, {}
+        for step in range(BLOCKS + 2):
+            if step < BLOCKS:
+                made = order[step]
+                g, half = made
                 block = g * HALVES + half
                 rows = slice(block * P, (block + 1) * P)
-                proj_ps = proj_banks.tile([P, BASINS], F32, name="proj_ps")
+                proj_ps = banks.tile([P, BASINS], F32, name="proj_ps", tag="bank")
                 nc.tensor.matmul(proj_ps[:], w_emb_sb[:, rows], emb_bf[:], start=True, stop=True)
-                proj = held.tile([P, BASINS], F32, name=f"proj{block}")
-                nc.scalar.copy(proj[:], proj_ps[:])
-                q_ps = q_banks.tile([P, SAMPLES], F32, name="q_ps")
+                proj[made] = held.tile([P, BASINS], F32, name=f"proj{block}")
+                nc.scalar.copy(proj[made][:], proj_ps[:])
+                q_ps = banks.tile([P, SAMPLES], F32, name="q_ps", tag="bank")
                 nc.tensor.matmul(q_ps[:], w_feat_sb[:, rows], wf_bf[:], start=True, stop=True)
-                q = work.tile([P, SAMPLES], F32, name=f"q{g}")
-                nc.vector.tensor_scalar_add(q[:], q_ps[:], bias[:, block : block + 1])
-                a = work.tile([P, SAMPLES], F32, name=f"a{g}")
-                nc.vector.tensor_tensor(a[:], proj[:].indirect(offsets[:]), q[:], ALU.add)
-                acted = work.tile([P, SAMPLES], F32, name=f"gate{g}")
-                nc.scalar.activation(acted[:], a[:], functions[g])
-                gate.append(acted)
-            cell = work.tile([P, SAMPLES], F32, name="cell")
-            nc.gpsimd.tensor_tensor(cell[:], gate[0][:], gate[1][:], ALU.mult)
-            cell_tanh = work.tile([P, SAMPLES], F32, name="cell_tanh")
-            nc.scalar.activation(cell_tanh[:], cell[:], ACT.Tanh)
-            hidden = work.tile([P, SAMPLES], F32, name="hidden")
-            nc.vector.tensor_tensor(hidden[:], gate[2][:], cell_tanh[:], ALU.mult)
-            nc.sync.dma_start(out[half * P : (half + 1) * P, :], hidden[:])
+                q[made] = held.tile([P, SAMPLES], F32, name=f"q{block}")
+                nc.vector.tensor_scalar_add(q[made][:], q_ps[:], bias[:, block : block + 1])
+            if 1 <= step <= BLOCKS:
+                looked_up = order[step - 1]
+                g, half = looked_up
+                a[looked_up] = held.tile([P, SAMPLES], F32, name=f"a{g}{half}")
+                nc.vector.tensor_tensor(
+                    a[looked_up][:],
+                    proj[looked_up][:].indirect(offsets[:]),
+                    q[looked_up][:],
+                    ALU.add,
+                )
+            if step >= 2:
+                applied = order[step - 2]
+                g, half = applied
+                gate[applied] = held.tile([P, SAMPLES], F32, name=f"gate{g}{half}")
+                nc.scalar.activation(gate[applied][:], a[applied][:], functions[g])
+                if g == CANDIDATE:
+                    cell = held.tile([P, SAMPLES], F32, name=f"cell{half}")
+                    nc.vector.tensor_tensor(
+                        cell[:], gate[(INPUT, half)][:], gate[applied][:], ALU.mult
+                    )
+                    cell_tanh[half] = held.tile([P, SAMPLES], F32, name=f"cell_tanh{half}")
+                    nc.scalar.activation(cell_tanh[half][:], cell[:], ACT.Tanh)
+                if g == OUTPUT:
+                    hidden = held.tile([P, SAMPLES], F32, name=f"hidden{half}")
+                    nc.vector.tensor_tensor(
+                        hidden[:], gate[applied][:], cell_tanh[half][:], ALU.mult
+                    )
+                    nc.sync.dma_start(out[half * P : (half + 1) * P, :], hidden[:])

@@ -16,7 +16,6 @@ SAMPLES = 256
 HALVES = HIDDEN // P
 BLOCKS = GATES * HALVES
 PSUM_BANKS = 8
-WARM_MATMULS = 6
 CLIP = 3.0
 WEIGHT_CAP = 0.5
 
@@ -48,11 +47,6 @@ def tile_sca2lstm_kernel(tc, emb, w_emb, sf, wgt, w_feat, b, offs, out):
         scratch_out = held.tile([P, 1], F32, name="scratch_out")
         nc.vector.memset(scratch_in[:], 0.0)
         nc.scalar.activation(scratch_out[:], scratch_in[:], ACT.Sigmoid)
-        zeros = held.tile([P, BASINS], BF16, name="zeros")
-        nc.vector.memset(zeros[:], 0.0)
-        unread_ps = banks.tile([P, BASINS], F32, name="unread_ps", tag="bank")
-        for repeat in range(WARM_MATMULS):
-            nc.tensor.matmul(unread_ps[:], zeros[:, 0:P], zeros[:], start=True, stop=True)
 
         sf_clipped = held.tile([P, SAMPLES], F32, name="sf_clipped")
         nc.vector.tensor_scalar(sf_clipped[:], sf_f32[:], -CLIP, CLIP, ALU.max, ALU.min)

@@ -16,6 +16,7 @@ SAMPLES = 256
 HALVES = HIDDEN // P
 BLOCKS = GATES * HALVES
 PSUM_BANKS = 8
+WARM_MATMULS = 6
 CLIP = 3.0
 WEIGHT_CAP = 0.5
 
@@ -32,12 +33,12 @@ def tile_sca2lstm_kernel(tc, emb, w_emb, sf, wgt, w_feat, b, offs, out):
         nc.sync.dma_start(emb_f32[:], emb)
         sf_f32 = held.tile([P, SAMPLES], F32, name="sf_f32")
         nc.scalar.dma_start(sf_f32[:], sf)
-        b_rows = held.tile([BLOCKS, P], F32, name="b_rows")
-        nc.gpsimd.dma_start(b_rows[:], b.rearrange("(k p) o -> k (p o)", p=P))
         w_emb_sb = held.tile([P, BLOCKS * P], BF16, name="w_emb_sb")
         nc.sync.dma_start(w_emb_sb[:], w_emb)
         wgt_f32 = held.tile([P, SAMPLES], F32, name="wgt_f32")
         nc.scalar.dma_start(wgt_f32[:], wgt)
+        b_rows = held.tile([BLOCKS, P], F32, name="b_rows")
+        nc.sync.dma_start(b_rows[:], b.rearrange("(k p) o -> k (p o)", p=P))
         offsets = held.tile([P, SAMPLES // 16], U16, name="offsets")
         nc.sync.dma_start(offsets[:], offs)
         w_feat_sb = held.tile([P, BLOCKS * P], BF16, name="w_feat_sb")
@@ -47,6 +48,11 @@ def tile_sca2lstm_kernel(tc, emb, w_emb, sf, wgt, w_feat, b, offs, out):
         scratch_out = held.tile([P, 1], F32, name="scratch_out")
         nc.vector.memset(scratch_in[:], 0.0)
         nc.scalar.activation(scratch_out[:], scratch_in[:], ACT.Sigmoid)
+        zeros = held.tile([P, BASINS], BF16, name="zeros")
+        nc.vector.memset(zeros[:], 0.0)
+        unread_ps = banks.tile([P, BASINS], F32, name="unread_ps", tag="bank")
+        for repeat in range(WARM_MATMULS):
+            nc.tensor.matmul(unread_ps[:], zeros[:, 0:P], zeros[:], start=True, stop=True)
 
         sf_clipped = held.tile([P, SAMPLES], F32, name="sf_clipped")
         nc.vector.tensor_scalar(sf_clipped[:], sf_f32[:], -CLIP, CLIP, ALU.max, ALU.min)

@@ -67,8 +67,6 @@ def tile_sca2lstm_kernel(tc, emb, w_emb, sf, wgt, w_feat, b, offs, out):
         make_identity(nc, identity[:])
         bias_ps = banks.tile([P, BLOCKS], F32, name="bias_ps", tag="bank")
         nc.tensor.matmul(bias_ps[:], b_rows[:], identity[:], start=True, stop=True)
-        bias = held.tile([P, BLOCKS], F32, name="bias")
-        nc.vector.tensor_copy(bias[:], bias_ps[:])
 
         order = [(g, half) for half in range(HALVES) for g in (INPUT, CANDIDATE)]
         order += [(OUTPUT, half) for half in range(HALVES)]
@@ -87,7 +85,7 @@ def tile_sca2lstm_kernel(tc, emb, w_emb, sf, wgt, w_feat, b, offs, out):
                 q_ps = banks.tile([P, SAMPLES], F32, name="q_ps", tag="bank")
                 nc.tensor.matmul(q_ps[:], w_feat_sb[:, rows], wf_bf[:], start=True, stop=True)
                 q[made] = held.tile([P, SAMPLES], F32, name=f"q{block}")
-                nc.vector.tensor_scalar_add(q[made][:], q_ps[:], bias[:, block : block + 1])
+                nc.vector.tensor_scalar_add(q[made][:], q_ps[:], bias_ps[:, block : block + 1])
             if 1 <= step <= BLOCKS:
                 looked_up = order[step - 1]
                 g, half = looked_up

@@ -1,5 +1,4 @@
 import concourse.mybir as mybir
-from concourse.masks import make_identity
 
 F32 = mybir.dt.float32
 BF16 = mybir.dt.bfloat16
@@ -16,7 +15,7 @@ SAMPLES = 256
 HALVES = HIDDEN // P
 BLOCKS = GATES * HALVES
 PSUM_BANKS = 8
-WARM_MATMULS = 6
+WARM_MATMULS = 4
 CLIP = 3.0
 WEIGHT_CAP = 0.5
 
@@ -31,18 +30,18 @@ def tile_sca2lstm_kernel(tc, emb, w_emb, sf, wgt, w_feat, b, offs, out):
     ):
         emb_f32 = held.tile([P, BASINS], F32, name="emb_f32")
         nc.sync.dma_start(emb_f32[:], emb)
-        sf_f32 = held.tile([P, SAMPLES], F32, name="sf_f32")
-        nc.scalar.dma_start(sf_f32[:], sf)
         w_emb_sb = held.tile([P, BLOCKS * P], BF16, name="w_emb_sb")
-        nc.sync.dma_start(w_emb_sb[:], w_emb)
+        nc.scalar.dma_start(w_emb_sb[:], w_emb)
+        sf_f32 = held.tile([P, SAMPLES], F32, name="sf_f32")
+        nc.sync.dma_start(sf_f32[:], sf)
         wgt_f32 = held.tile([P, SAMPLES], F32, name="wgt_f32")
         nc.scalar.dma_start(wgt_f32[:], wgt)
-        b_rows = held.tile([BLOCKS, P], F32, name="b_rows")
-        nc.sync.dma_start(b_rows[:], b.rearrange("(k p) o -> k (p o)", p=P))
+        w_feat_sb = held.tile([P, BLOCKS * P], BF16, name="w_feat_sb")
+        nc.sync.dma_start(w_feat_sb[:], w_feat)
         offsets = held.tile([P, SAMPLES // 16], U16, name="offsets")
         nc.sync.dma_start(offsets[:], offs)
-        w_feat_sb = held.tile([P, BLOCKS * P], BF16, name="w_feat_sb")
-        nc.scalar.dma_start(w_feat_sb[:], w_feat)
+        bias = held.tile([P, BLOCKS], F32, name="bias")
+        nc.sync.dma_start(bias[:], b.rearrange("(k p) o -> p (k o)", p=P))
 
         scratch_in = held.tile([P, 1], F32, name="scratch_in")
         scratch_out = held.tile([P, 1], F32, name="scratch_out")
@@ -54,19 +53,14 @@ def tile_sca2lstm_kernel(tc, emb, w_emb, sf, wgt, w_feat, b, offs, out):
         for repeat in range(WARM_MATMULS):
             nc.tensor.matmul(unread_ps[:], zeros[:, 0:P], zeros[:], start=True, stop=True)
 
-        sf_clipped = held.tile([P, SAMPLES], F32, name="sf_clipped")
-        nc.vector.tensor_scalar(sf_clipped[:], sf_f32[:], -CLIP, CLIP, ALU.max, ALU.min)
         emb_bf = held.tile([P, BASINS], BF16, name="emb_bf")
         nc.vector.tensor_scalar(emb_bf[:], emb_f32[:], -CLIP, CLIP, ALU.max, ALU.min)
+        sf_clipped = held.tile([P, SAMPLES], F32, name="sf_clipped")
+        nc.vector.tensor_scalar(sf_clipped[:], sf_f32[:], -CLIP, CLIP, ALU.max, ALU.min)
         wf_bf = held.tile([P, SAMPLES], BF16, name="wf_bf")
         nc.vector.scalar_tensor_tensor(
             wf_bf[:], wgt_f32[:], WEIGHT_CAP, sf_clipped[:], ALU.min, ALU.mult
         )
-
-        identity = held.tile([BLOCKS, BLOCKS], F32, name="identity")
-        make_identity(nc, identity[:])
-        bias_ps = banks.tile([P, BLOCKS], F32, name="bias_ps", tag="bank")
-        nc.tensor.matmul(bias_ps[:], b_rows[:], identity[:], start=True, stop=True)
 
         order = [(g, half) for half in range(HALVES) for g in (INPUT, CANDIDATE)]
         order += [(OUTPUT, half) for half in range(HALVES)]
@@ -85,7 +79,7 @@ def tile_sca2lstm_kernel(tc, emb, w_emb, sf, wgt, w_feat, b, offs, out):
                 q_ps = banks.tile([P, SAMPLES], F32, name="q_ps", tag="bank")
                 nc.tensor.matmul(q_ps[:], w_feat_sb[:, rows], wf_bf[:], start=True, stop=True)
                 q[made] = held.tile([P, SAMPLES], F32, name=f"q{block}")
-                nc.vector.tensor_scalar_add(q[made][:], q_ps[:], bias_ps[:, block : block + 1])
+                nc.vector.tensor_copy(q[made][:], q_ps[:])
             if 1 <= step <= BLOCKS:
                 looked_up = order[step - 1]
                 g, half = looked_up
@@ -100,7 +94,10 @@ def tile_sca2lstm_kernel(tc, emb, w_emb, sf, wgt, w_feat, b, offs, out):
                 applied = order[step - 2]
                 g, half = applied
                 gate[applied] = held.tile([P, SAMPLES], F32, name=f"gate{g}{half}")
-                nc.scalar.activation(gate[applied][:], a[applied][:], functions[g])
+                block = g * HALVES + half
+                nc.scalar.activation(
+                    gate[applied][:], a[applied][:], functions[g], bias=bias[:, block : block + 1]
+                )
                 if g == CANDIDATE:
                     cell = held.tile([P, SAMPLES], F32, name=f"cell{half}")
                     nc.vector.tensor_tensor(

@@ -41,7 +41,7 @@ def tile_sca2lstm_kernel(tc, emb, w_emb, sf, wgt, w_feat, b, offs, out):
         offsets = held.tile([P, SAMPLES // 16], U16, name="offsets")
         nc.sync.dma_start(offsets[:], offs)
         bias = held.tile([P, BLOCKS], F32, name="bias")
-        nc.sync.dma_start(bias[:], b.rearrange("(k p) o -> p (k o)", p=P))
+        nc.gpsimd.dma_start(bias[:], b.rearrange("(k p) o -> p (k o)", p=P))
 
         scratch_in = held.tile([P, 1], F32, name="scratch_in")
         scratch_out = held.tile([P, 1], F32, name="scratch_out")

@@ -31,11 +31,11 @@ def tile_sca2lstm_kernel(tc, emb, w_emb, sf, wgt, w_feat, b, offs, out):
         emb_f32 = held.tile([P, BASINS], F32, name="emb_f32")
         nc.sync.dma_start(emb_f32[:], emb)
         w_emb_sb = held.tile([P, BLOCKS * P], BF16, name="w_emb_sb")
-        nc.scalar.dma_start(w_emb_sb[:], w_emb)
+        nc.sync.dma_start(w_emb_sb[:], w_emb)
         sf_f32 = held.tile([P, SAMPLES], F32, name="sf_f32")
         nc.sync.dma_start(sf_f32[:], sf)
         wgt_f32 = held.tile([P, SAMPLES], F32, name="wgt_f32")
-        nc.scalar.dma_start(wgt_f32[:], wgt)
+        nc.sync.dma_start(wgt_f32[:], wgt)
         w_feat_sb = held.tile([P, BLOCKS * P], BF16, name="w_feat_sb")
         nc.sync.dma_start(w_feat_sb[:], w_feat)
         offsets = held.tile([P, SAMPLES // 16], U16, name="offsets")

@@ -28,16 +28,16 @@ def tile_sca2lstm_kernel(tc, emb, w_emb, sf, wgt, w_feat, b, offs, out):
         tc.tile_pool(name="held", bufs=1) as held,
         tc.psum_pool(name="banks", bufs=PSUM_BANKS) as banks,
     ):
-        emb_f32 = held.tile([P, BASINS], F32, name="emb_f32")
-        nc.sync.dma_start(emb_f32[:], emb)
-        w_emb_sb = held.tile([P, BLOCKS * P], BF16, name="w_emb_sb")
-        nc.sync.dma_start(w_emb_sb[:], w_emb)
         sf_f32 = held.tile([P, SAMPLES], F32, name="sf_f32")
         nc.sync.dma_start(sf_f32[:], sf)
         wgt_f32 = held.tile([P, SAMPLES], F32, name="wgt_f32")
         nc.sync.dma_start(wgt_f32[:], wgt)
         w_feat_sb = held.tile([P, BLOCKS * P], BF16, name="w_feat_sb")
         nc.sync.dma_start(w_feat_sb[:], w_feat)
+        emb_f32 = held.tile([P, BASINS], F32, name="emb_f32")
+        nc.sync.dma_start(emb_f32[:], emb)
+        w_emb_sb = held.tile([P, BLOCKS * P], BF16, name="w_emb_sb")
+        nc.sync.dma_start(w_emb_sb[:], w_emb)
         offsets = held.tile([P, SAMPLES // 16], U16, name="offsets")
         nc.sync.dma_start(offsets[:], offs)
         bias = held.tile([P, BLOCKS], F32, name="bias")
@@ -53,33 +53,55 @@ def tile_sca2lstm_kernel(tc, emb, w_emb, sf, wgt, w_feat, b, offs, out):
         for repeat in range(WARM_MATMULS):
             nc.tensor.matmul(unread_ps[:], zeros[:, 0:P], zeros[:], start=True, stop=True)
 
-        emb_bf = held.tile([P, BASINS], BF16, name="emb_bf")
-        nc.vector.tensor_scalar(emb_bf[:], emb_f32[:], -CLIP, CLIP, ALU.max, ALU.min)
+        order = [(g, half) for half in range(HALVES) for g in (INPUT, CANDIDATE)]
+        order += [(OUTPUT, half) for half in range(HALVES)]
+
         sf_clipped = held.tile([P, SAMPLES], F32, name="sf_clipped")
         nc.vector.tensor_scalar(sf_clipped[:], sf_f32[:], -CLIP, CLIP, ALU.max, ALU.min)
         wf_bf = held.tile([P, SAMPLES], BF16, name="wf_bf")
         nc.vector.scalar_tensor_tensor(
             wf_bf[:], wgt_f32[:], WEIGHT_CAP, sf_clipped[:], ALU.min, ALU.mult
         )
+        q = {}
+        pairs = [order[first : first + 2] for first in range(0, BLOCKS, 2)]
+        emb_bf = held.tile([P, BASINS], BF16, name="emb_bf")
+        for number, pair in enumerate(pairs):
+            q_ps = banks.tile([P, 2 * SAMPLES], F32, name="q_ps", tag="bank")
+            q_sb = held.tile([P, 2 * SAMPLES], F32, name=f"q_sb{number}")
+            for side, (g, half) in enumerate(pair):
+                block = g * HALVES + half
+                columns = slice(side * SAMPLES, (side + 1) * SAMPLES)
+                nc.tensor.matmul(
+                    q_ps[:, columns],
+                    w_feat_sb[:, block * P : (block + 1) * P],
+                    wf_bf[:],
+                    start=True,
+                    stop=True,
+                )
+                q[(g, half)] = q_sb[:, columns]
+            if number < len(pairs) - 1:
+                nc.scalar.copy(q_sb[:], q_ps[:])
+            else:
+                nc.vector.tensor_scalar(emb_bf[:], emb_f32[:], -CLIP, CLIP, ALU.max, ALU.min)
+                nc.vector.tensor_copy(q_sb[:], q_ps[:])
 
-        order = [(g, half) for half in range(HALVES) for g in (INPUT, CANDIDATE)]
-        order += [(OUTPUT, half) for half in range(HALVES)]
         functions = {INPUT: ACT.Sigmoid, CANDIDATE: ACT.Tanh, OUTPUT: ACT.Sigmoid}
-        proj, q, a, gate, cell_tanh = {}, {}, {}, {}, {}
+        proj, a, gate, cell_tanh = {}, {}, {}, {}
         for step in range(BLOCKS + 2):
             if step < BLOCKS:
                 made = order[step]
                 g, half = made
                 block = g * HALVES + half
-                rows = slice(block * P, (block + 1) * P)
                 proj_ps = banks.tile([P, BASINS], F32, name="proj_ps", tag="bank")
-                nc.tensor.matmul(proj_ps[:], w_emb_sb[:, rows], emb_bf[:], start=True, stop=True)
+                nc.tensor.matmul(
+                    proj_ps[:], w_emb_sb[:, block * P : (block + 1) * P], emb_bf[:],
+                    start=True, stop=True,
+                )
                 proj[made] = held.tile([P, BASINS], F32, name=f"proj{block}")
-                nc.scalar.copy(proj[made][:], proj_ps[:])
-                q_ps = banks.tile([P, SAMPLES], F32, name="q_ps", tag="bank")
-                nc.tensor.matmul(q_ps[:], w_feat_sb[:, rows], wf_bf[:], start=True, stop=True)
-                q[made] = held.tile([P, SAMPLES], F32, name=f"q{block}")
-                nc.vector.tensor_copy(q[made][:], q_ps[:])
+                if step == 1:
+                    nc.vector.tensor_copy(proj[made][:], proj_ps[:])
+                else:
+                    nc.scalar.copy(proj[made][:], proj_ps[:])
             if 1 <= step <= BLOCKS:
                 looked_up = order[step - 1]
                 g, half = looked_up
@@ -87,7 +109,7 @@ def tile_sca2lstm_kernel(tc, emb, w_emb, sf, wgt, w_feat, b, offs, out):
                 nc.vector.tensor_tensor(
                     a[looked_up][:],
                     proj[looked_up][:].indirect(offsets[:]),
-                    q[looked_up][:],
+                    q[looked_up],
                     ALU.add,
                 )
             if step >= 2:

@@ -1,4 +1,5 @@
 import concourse.mybir as mybir
+from concourse.masks import make_identity
 
 F32 = mybir.dt.float32
 BF16 = mybir.dt.bfloat16
@@ -40,8 +41,10 @@ def tile_sca2lstm_kernel(tc, emb, w_emb, sf, wgt, w_feat, b, offs, out):
         nc.sync.dma_start(w_emb_sb[:], w_emb)
         offsets = held.tile([P, SAMPLES // 16], U16, name="offsets")
         nc.sync.dma_start(offsets[:], offs)
-        bias = held.tile([P, BLOCKS], F32, name="bias")
-        nc.gpsimd.dma_start(bias[:], b.rearrange("(k p) o -> p (k o)", p=P))
+        b_rows = held.tile([BLOCKS, P], F32, name="b_rows")
+        nc.gpsimd.dma_start(b_rows[:], b.rearrange("(k p) o -> k (p o)", p=P))
+        identity = held.tile([BLOCKS, BLOCKS], F32, name="identity")
+        make_identity(nc, identity[:])
 
         scratch_in = held.tile([P, 1], F32, name="scratch_in")
         scratch_out = held.tile([P, 1], F32, name="scratch_out")
@@ -87,23 +90,28 @@ def tile_sca2lstm_kernel(tc, emb, w_emb, sf, wgt, w_feat, b, offs, out):
 
         functions = {INPUT: ACT.Sigmoid, CANDIDATE: ACT.Tanh, OUTPUT: ACT.Sigmoid}
         proj, a, gate, cell_tanh = {}, {}, {}, {}
-        for step in range(BLOCKS + 2):
+        for step, made in enumerate(order):
+            g, half = made
+            block = g * HALVES + half
+            proj_ps = banks.tile([P, BASINS], F32, name="proj_ps", tag="bank")
+            nc.tensor.matmul(
+                proj_ps[:], w_emb_sb[:, block * P : (block + 1) * P], emb_bf[:],
+                start=True, stop=True,
+            )
+            proj[made] = held.tile([P, BASINS], F32, name=f"proj{block}")
+            if step == 1:
+                nc.vector.tensor_copy(proj[made][:], proj_ps[:])
+            else:
+                nc.scalar.copy(proj[made][:], proj_ps[:])
+
+        bias_ps = banks.tile([P, BLOCKS], F32, name="bias_ps", tag="bank")
+        nc.tensor.matmul(bias_ps[:], b_rows[:], identity[:], start=True, stop=True)
+        bias = held.tile([P, BLOCKS], F32, name="bias")
+        nc.scalar.copy(bias[:], bias_ps[:])
+
+        for step in range(BLOCKS + 1):
             if step < BLOCKS:
-                made = order[step]
-                g, half = made
-                block = g * HALVES + half
-                proj_ps = banks.tile([P, BASINS], F32, name="proj_ps", tag="bank")
-                nc.tensor.matmul(
-                    proj_ps[:], w_emb_sb[:, block * P : (block + 1) * P], emb_bf[:],
-                    start=True, stop=True,
-                )
-                proj[made] = held.tile([P, BASINS], F32, name=f"proj{block}")
-                if step == 1:
-                    nc.vector.tensor_copy(proj[made][:], proj_ps[:])
-                else:
-                    nc.scalar.copy(proj[made][:], proj_ps[:])
-            if 1 <= step <= BLOCKS:
-                looked_up = order[step - 1]
+                looked_up = order[step]
                 g, half = looked_up
                 a[looked_up] = held.tile([P, SAMPLES], F32, name=f"a{g}{half}")
                 nc.vector.tensor_tensor(
@@ -112,8 +120,8 @@ def tile_sca2lstm_kernel(tc, emb, w_emb, sf, wgt, w_feat, b, offs, out):
                     q[looked_up],
                     ALU.add,
                 )
-            if step >= 2:
-                applied = order[step - 2]
+            if step >= 1:
+                applied = order[step - 1]
                 g, half = applied
                 gate[applied] = held.tile([P, SAMPLES], F32, name=f"gate{g}{half}")
                 block = g * HALVES + half

@@ -65,9 +65,10 @@ def tile_sca2lstm_kernel(tc, emb, w_emb, sf, wgt, w_feat, b, offs, out):
         nc.vector.scalar_tensor_tensor(
             wf_bf[:], wgt_f32[:], WEIGHT_CAP, sf_clipped[:], ALU.min, ALU.mult
         )
+        emb_bf = held.tile([P, BASINS], BF16, name="emb_bf")
+        nc.vector.tensor_scalar(emb_bf[:], emb_f32[:], -CLIP, CLIP, ALU.max, ALU.min)
         q = {}
         pairs = [order[first : first + 2] for first in range(0, BLOCKS, 2)]
-        emb_bf = held.tile([P, BASINS], BF16, name="emb_bf")
         for number, pair in enumerate(pairs):
             q_ps = banks.tile([P, 2 * SAMPLES], F32, name="q_ps", tag="bank")
             q_sb = held.tile([P, 2 * SAMPLES], F32, name=f"q_sb{number}")
@@ -82,10 +83,9 @@ def tile_sca2lstm_kernel(tc, emb, w_emb, sf, wgt, w_feat, b, offs, out):
                     stop=True,
                 )
                 q[(g, half)] = q_sb[:, columns]
-            if number < len(pairs) - 1:
+            if number == 0:
                 nc.scalar.copy(q_sb[:], q_ps[:])
             else:
-                nc.vector.tensor_scalar(emb_bf[:], emb_f32[:], -CLIP, CLIP, ALU.max, ALU.min)
                 nc.vector.tensor_copy(q_sb[:], q_ps[:])
 
         functions = {INPUT: ACT.Sigmoid, CANDIDATE: ACT.Tanh, OUTPUT: ACT.Sigmoid}

@@ -68,25 +68,18 @@ def tile_sca2lstm_kernel(tc, emb, w_emb, sf, wgt, w_feat, b, offs, out):
         emb_bf = held.tile([P, BASINS], BF16, name="emb_bf")
         nc.vector.tensor_scalar(emb_bf[:], emb_f32[:], -CLIP, CLIP, ALU.max, ALU.min)
         q = {}
-        pairs = [order[first : first + 2] for first in range(0, BLOCKS, 2)]
-        for number, pair in enumerate(pairs):
-            q_ps = banks.tile([P, 2 * SAMPLES], F32, name="q_ps", tag="bank")
-            q_sb = held.tile([P, 2 * SAMPLES], F32, name=f"q_sb{number}")
-            for side, (g, half) in enumerate(pair):
-                block = g * HALVES + half
-                columns = slice(side * SAMPLES, (side + 1) * SAMPLES)
-                nc.tensor.matmul(
-                    q_ps[:, columns],
-                    w_feat_sb[:, block * P : (block + 1) * P],
-                    wf_bf[:],
-                    start=True,
-                    stop=True,
-                )
-                q[(g, half)] = q_sb[:, columns]
-            if number == 0:
+        for number, (g, half) in enumerate(order):
+            block = g * HALVES + half
+            q_ps = banks.tile([P, SAMPLES], F32, name="q_ps", tag="bank")
+            nc.tensor.matmul(
+                q_ps[:], w_feat_sb[:, block * P : (block + 1) * P], wf_bf[:], start=True, stop=True
+            )
+            q_sb = held.tile([P, SAMPLES], F32, name=f"q_sb{block}")
+            if number < BLOCKS // 2:
                 nc.scalar.copy(q_sb[:], q_ps[:])
             else:
                 nc.vector.tensor_copy(q_sb[:], q_ps[:])
+            q[(g, half)] = q_sb[:]
 
         functions = {INPUT: ACT.Sigmoid, CANDIDATE: ACT.Tanh, OUTPUT: ACT.Sigmoid}
         proj, a, gate, cell_tanh = {}, {}, {}, {}

@@ -1,5 +1,4 @@
 import concourse.mybir as mybir
-from concourse.masks import make_identity
 
 F32 = mybir.dt.float32
 BF16 = mybir.dt.bfloat16
@@ -41,10 +40,8 @@ def tile_sca2lstm_kernel(tc, emb, w_emb, sf, wgt, w_feat, b, offs, out):
         nc.sync.dma_start(w_emb_sb[:], w_emb)
         offsets = held.tile([P, SAMPLES // 16], U16, name="offsets")
         nc.sync.dma_start(offsets[:], offs)
-        b_rows = held.tile([BLOCKS, P], F32, name="b_rows")
-        nc.gpsimd.dma_start(b_rows[:], b.rearrange("(k p) o -> k (p o)", p=P))
-        identity = held.tile([BLOCKS, BLOCKS], F32, name="identity")
-        make_identity(nc, identity[:])
+        bias = held.tile([P, BLOCKS], F32, name="bias")
+        nc.gpsimd.dma_start(bias[:], b.rearrange("(k p) o -> p (k o)", p=P))
 
         scratch_in = held.tile([P, 1], F32, name="scratch_in")
         scratch_out = held.tile([P, 1], F32, name="scratch_out")
@@ -96,11 +93,6 @@ def tile_sca2lstm_kernel(tc, emb, w_emb, sf, wgt, w_feat, b, offs, out):
                 nc.vector.tensor_copy(proj[made][:], proj_ps[:])
             else:
                 nc.scalar.copy(proj[made][:], proj_ps[:])
-
-        bias_ps = banks.tile([P, BLOCKS], F32, name="bias_ps", tag="bank")
-        nc.tensor.matmul(bias_ps[:], b_rows[:], identity[:], start=True, stop=True)
-        bias = held.tile([P, BLOCKS], F32, name="bias")
-        nc.scalar.copy(bias[:], bias_ps[:])
 
         for step in range(BLOCKS + 1):
             if step < BLOCKS:

import concourse.mybir as mybir

F32 = mybir.dt.float32
BF16 = mybir.dt.bfloat16
U16 = mybir.dt.uint16
ALU = mybir.AluOpType
ACT = mybir.ActivationFunctionType

P = 128
HIDDEN = 256
GATES = 3
INPUT, CANDIDATE, OUTPUT = 0, 1, 2
BASINS = 512
SAMPLES = 256
HALVES = HIDDEN // P
BLOCKS = GATES * HALVES
PSUM_BANKS = 8
WARM_MATMULS = 4
CLIP = 3.0
WEIGHT_CAP = 0.5

FLOPS = 2 * P * GATES * HIDDEN * (BASINS + SAMPLES)


def tile_sca2lstm_kernel(tc, emb, w_emb, sf, wgt, w_feat, b, offs, out):
    nc = tc.nc
    with (
        tc.tile_pool(name="held", bufs=1) as held,
        tc.psum_pool(name="banks", bufs=PSUM_BANKS) as banks,
    ):
        sf_f32 = held.tile([P, SAMPLES], F32, name="sf_f32")
        nc.sync.dma_start(sf_f32[:], sf)
        wgt_f32 = held.tile([P, SAMPLES], F32, name="wgt_f32")
        nc.sync.dma_start(wgt_f32[:], wgt)
        w_feat_sb = held.tile([P, BLOCKS * P], BF16, name="w_feat_sb")
        nc.sync.dma_start(w_feat_sb[:], w_feat)
        emb_f32 = held.tile([P, BASINS], F32, name="emb_f32")
        nc.sync.dma_start(emb_f32[:], emb)
        w_emb_sb = held.tile([P, BLOCKS * P], BF16, name="w_emb_sb")
        nc.sync.dma_start(w_emb_sb[:], w_emb)
        offsets = held.tile([P, SAMPLES // 16], U16, name="offsets")
        nc.sync.dma_start(offsets[:], offs)
        bias = held.tile([P, BLOCKS], F32, name="bias")
        nc.gpsimd.dma_start(bias[:], b.rearrange("(k p) o -> p (k o)", p=P))

        scratch_in = held.tile([P, 1], F32, name="scratch_in")
        scratch_out = held.tile([P, 1], F32, name="scratch_out")
        nc.vector.memset(scratch_in[:], 0.0)
        nc.scalar.activation(scratch_out[:], scratch_in[:], ACT.Sigmoid)
        zeros = held.tile([P, BASINS], BF16, name="zeros")
        nc.vector.memset(zeros[:], 0.0)
        unread_ps = banks.tile([P, BASINS], F32, name="unread_ps", tag="bank")
        for repeat in range(WARM_MATMULS):
            nc.tensor.matmul(unread_ps[:], zeros[:, 0:P], zeros[:], start=True, stop=True)

        order = [(g, half) for half in range(HALVES) for g in (INPUT, CANDIDATE)]
        order += [(OUTPUT, half) for half in range(HALVES)]

        sf_clipped = held.tile([P, SAMPLES], F32, name="sf_clipped")
        nc.vector.tensor_scalar(sf_clipped[:], sf_f32[:], -CLIP, CLIP, ALU.max, ALU.min)
        wf_bf = held.tile([P, SAMPLES], BF16, name="wf_bf")
        nc.vector.scalar_tensor_tensor(
            wf_bf[:], wgt_f32[:], WEIGHT_CAP, sf_clipped[:], ALU.min, ALU.mult
        )
        emb_bf = held.tile([P, BASINS], BF16, name="emb_bf")
        nc.vector.tensor_scalar(emb_bf[:], emb_f32[:], -CLIP, CLIP, ALU.max, ALU.min)
        q = {}
        for number, (g, half) in enumerate(order):
            block = g * HALVES + half
            q_ps = banks.tile([P, SAMPLES], F32, name="q_ps", tag="bank")
            nc.tensor.matmul(
                q_ps[:], w_feat_sb[:, block * P : (block + 1) * P], wf_bf[:], start=True, stop=True
            )
            q_sb = held.tile([P, SAMPLES], F32, name=f"q_sb{block}")
            if number < BLOCKS // 2:
                nc.scalar.copy(q_sb[:], q_ps[:])
            else:
                nc.vector.tensor_copy(q_sb[:], q_ps[:])
            q[(g, half)] = q_sb[:]

        functions = {INPUT: ACT.Sigmoid, CANDIDATE: ACT.Tanh, OUTPUT: ACT.Sigmoid}
        proj, a, gate, cell_tanh = {}, {}, {}, {}
        for step, made in enumerate(order):
            g, half = made
            block = g * HALVES + half
            proj_ps = banks.tile([P, BASINS], F32, name="proj_ps", tag="bank")
            nc.tensor.matmul(
                proj_ps[:], w_emb_sb[:, block * P : (block + 1) * P], emb_bf[:],
                start=True, stop=True,
            )
            proj[made] = held.tile([P, BASINS], F32, name=f"proj{block}")
            if step == 1:
                nc.vector.tensor_copy(proj[made][:], proj_ps[:])
            else:
                nc.scalar.copy(proj[made][:], proj_ps[:])

        for step in range(BLOCKS + 1):
            if step < BLOCKS:
                looked_up = order[step]
                g, half = looked_up
                a[looked_up] = held.tile([P, SAMPLES], F32, name=f"a{g}{half}")
                nc.vector.tensor_tensor(
                    a[looked_up][:],
                    proj[looked_up][:].indirect(offsets[:]),
                    q[looked_up],
                    ALU.add,
                )
            if step >= 1:
                applied = order[step - 1]
                g, half = applied
                gate[applied] = held.tile([P, SAMPLES], F32, name=f"gate{g}{half}")
                block = g * HALVES + half
                nc.scalar.activation(
                    gate[applied][:], a[applied][:], functions[g], bias=bias[:, block : block + 1]
                )
                if g == CANDIDATE:
                    cell = held.tile([P, SAMPLES], F32, name=f"cell{half}")
                    nc.vector.tensor_tensor(
                        cell[:], gate[(INPUT, half)][:], gate[applied][:], ALU.mult
                    )
                    cell_tanh[half] = held.tile([P, SAMPLES], F32, name=f"cell_tanh{half}")
                    nc.scalar.activation(cell_tanh[half][:], cell[:], ACT.Tanh)
                if g == OUTPUT:
                    hidden = held.tile([P, SAMPLES], F32, name=f"hidden{half}")
                    nc.vector.tensor_tensor(
                        hidden[:], gate[applied][:], cell_tanh[half][:], ALU.mult
                    )
                    nc.sync.dma_start(out[half * P : (half + 1) * P, :], hidden[:])
